import numpy as np
import ml_dtypes


def mxq(x, axis, fmt="e4m3"):
    dtype, down = {"e4m3": (ml_dtypes.float8_e4m3fn, 7), "e5m2": (ml_dtypes.float8_e5m2, 14)}[fmt]
    v = np.moveaxis(np.asarray(x, np.float32).astype(ml_dtypes.bfloat16).astype(np.float64), axis, -1)
    blocks = v.reshape(v.shape[:-1] + (-1, 32))
    amax = np.abs(blocks).max(-1, keepdims=True)
    byte = np.maximum(np.where(amax > 0, np.frexp(amax)[1] - 1 + 127, 0) - down, 1)
    scale = np.exp2(byte - 127.0)
    codes = (blocks / scale).astype(np.float32).astype(dtype).astype(np.float64)
    return np.moveaxis((codes * scale).reshape(v.shape), -1, axis)


WIDE = False


def mx_kscale(k):
    if not WIDE:
        return np.ones(k)
    levels = np.array([30, -30])
    if k % 512:
        return np.exp2(np.random.permutation(np.resize(levels, k // 32))).repeat(32)
    a = np.empty((k // 512, 16))
    for p in range(k // 512):
        a[p, :8] = np.random.permutation(np.resize(levels, 8))
        for g in range(8):
            far = levels[np.abs(levels - a[p, g]) >= 10]
            a[p, g + 8] = far[np.random.randint(len(far))]
    return np.exp2(a.ravel()).repeat(32)


BF16 = ml_dtypes.bfloat16


def bf(x):
    return np.asarray(x, np.float32).astype(BF16)


def f64(x):
    return np.asarray(x).astype(np.float64)


E2M1 = np.array([0.0, 0.5, 1.0, 1.5, 2.0, 3.0, 4.0, 6.0, -0.0, -0.5, -1.0, -1.5, -2.0, -3.0, -4.0, -6.0])


def pack_weight(w, fmt):
    k, n = w.shape
    w = f64(bf(w)).reshape(k // 32, 32, n)
    amax = np.abs(w).max(1)
    if fmt == "e4m3":
        byte = np.frexp(amax)[1] - 1 + 127 - 7
    else:
        mant, ex = np.frexp(amax / 6.0)
        byte = np.where(mant > 0.5, ex, ex - 1) + 127
    byte = np.clip(np.where(amax > 0, byte, 1), 1, 254)
    scaled = (w * np.exp2(127.0 - byte)[:, None, :]).reshape(k, n).astype(np.float32)
    by_word = np.ascontiguousarray(scaled.reshape(k // 512, 128, 4, n).transpose(0, 1, 3, 2))
    if fmt == "e4m3":
        words = by_word.astype(ml_dtypes.float8_e4m3fn).view(np.uint8)
    else:
        c = by_word.astype(ml_dtypes.float4_e2m1fn).view(np.uint8) & 0xF
        words = c[..., 0::2] | (c[..., 1::2] << 4)
    return np.ascontiguousarray(words), np.ascontiguousarray(byte.astype(np.uint8).reshape(k // 512, 16, n))


def unpack_weight(words, scales, fmt):
    g, p, n, _ = words.shape
    if fmt == "e4m3":
        vals = np.ascontiguousarray(words).view(ml_dtypes.float8_e4m3fn).astype(np.float64)
    else:
        nib = np.empty((g, p, n, 4), np.uint8)
        nib[..., 0::2] = words & 0xF
        nib[..., 1::2] = words >> 4
        vals = E2M1[nib]
    vals = vals * np.repeat(np.exp2(scales.astype(np.float64) - 127.0), 8, axis=1)[..., None]
    return vals.transpose(0, 1, 3, 2).reshape(g * 512, n)

def pack4(w):
    words, scales = pack_weight(w, "e2m1")
    return words.reshape(words.shape[0], 128, -1), scales


def unpack4(words, scales):
    return unpack_weight(words.reshape(words.shape[0], 128, -1, 2), scales, "e2m1")


B, S, E, H, KVH, HD = 1, 512, 2048, 16, 4, 128
THETA = 10000.0


def apply_rope(t, cos, sin):
    x1, x2 = np.split(t, 2, axis=-1)
    c = cos[None, None, :, :]
    s = sin[None, None, :, :]
    return np.concatenate([x1 * c - x2 * s, x2 * c + x1 * s], axis=-1)


def setup_inputs():
    s = mx_kscale(E)
    inv_freq = 1.0 / THETA ** (np.arange(0, HD, 2) / HD)
    pos = np.random.randint(0, S) + np.arange(S)
    ang = pos[:, None] * inv_freq[None, :]
    x = bf(np.random.standard_normal((B, S, E)) * s)
    Wq = np.random.standard_normal((H * HD, E)) * 1.3 / np.sqrt(E) / s[None, :]
    Wq_words, Wq_scales = pack4(np.ascontiguousarray(Wq.T))
    bq = bf(np.random.standard_normal(H * HD) * 0.3)
    Wkv = np.random.standard_normal((2 * KVH * HD, E)) * 1.3 / np.sqrt(E) / s[None, :]
    Wkv_words, Wkv_scales = pack4(np.ascontiguousarray(Wkv.T))
    bkv = bf(np.random.standard_normal(2 * KVH * HD) * 0.3)
    return {"x": x,
            "Wq_words": Wq_words,
            "Wq_scales": Wq_scales,
            "bq": bq,
            "Wkv_words": Wkv_words,
            "Wkv_scales": Wkv_scales,
            "bkv": bkv,
            "cos": bf(np.cos(ang)),
            "sin": bf(np.sin(ang))}


def reference(x, Wq_words, Wq_scales, bq, Wkv_words, Wkv_scales, bkv, cos, sin):
    xq = mxq(f64(x), 2, "e5m2")
    q = (xq @ unpack4(Wq_words, Wq_scales)) + f64(bq)
    kv = (xq @ unpack4(Wkv_words, Wkv_scales)) + f64(bkv)
    k, v = np.split(kv, 2, axis=-1)
    q = q.reshape(B, S, H, HD).transpose(0, 2, 1, 3)
    k = k.reshape(B, S, KVH, HD).transpose(0, 2, 1, 3)
    v = v.reshape(B, S, KVH, HD).transpose(0, 2, 1, 3)
    q_rot = apply_rope(q, f64(cos), f64(sin))
    k_rot = apply_rope(k, f64(cos), f64(sin))
    return q_rot, k_rot, v

@@ -1,0 +1,249 @@
+from contextlib import ExitStack
+
+import concourse.mybir as mybir
+from concourse.masks import make_identity
+
+F32 = mybir.dt.float32
+BF16 = mybir.dt.bfloat16
+I32 = mybir.dt.int32
+U32 = mybir.dt.uint32
+U8 = mybir.dt.uint8
+E5M2X4 = mybir.dt.float8_e5m2_x4
+E2M1X4 = mybir.dt.float4_e2m1fn_x4
+ALU = mybir.AluOpType
+ACT = mybir.ActivationFunctionType
+
+P = 128
+PASSES = 4
+TOKEN_TILES = 4
+HALF = 64
+GPSIMD_BANKS = (3, 8, 13, 18)
+WARM_MATMULS = 6
+
+FLOPS = 2 * 512 * 2048 * 3072
+
+
+def tile_qwen2attention_pa_kernel(
+    tc, x, Wq_words, Wq_scales, bq, Wkv_words, Wkv_scales, bkv, cos, sin, out_0, out_1, out_2
+):
+    nc = tc.nc
+    with ExitStack() as ctx:
+        const = ctx.enter_context(tc.tile_pool(name="const", bufs=1))
+        work = ctx.enter_context(tc.tile_pool(name="work", bufs=4))
+        accp = ctx.enter_context(tc.psum_pool(name="accp", bufs=4))
+        auxp = ctx.enter_context(tc.psum_pool(name="auxp", bufs=4))
+
+        plane_cols = (512, 1536, 1024)
+        planes = [
+            const.tile([P, PASSES, plane_cols[i]], U8, name="plane%d" % i, align_bytes=64) for i in range(3)
+        ]
+        plane_src = (Wq_scales[:, :, 0:512], Wq_scales[:, :, 512:2048], Wkv_scales)
+        plane_of = ((0, 0), (1, 0), (1, 512), (1, 1024), (2, 0), (2, 512))
+        w = [const.tile([P, PASSES, 1024], U8, name="w%d" % c, align_bytes=64) for c in range(6)]
+        xs = [const.tile([P, 2048], BF16, name="xs%d" % m) for m in range(4)]
+        grouped = [
+            [const.tile([P, 1024], BF16, name="xg%d%d" % (m, gp), align_bytes=64) for gp in range(2)]
+            for m in range(4)
+        ]
+        xq = [[const.tile([P, 256], U32, name="xq%d%d" % (m, gp), align_bytes=64) for gp in range(2)] for m in range(4)]
+        xsc = [[const.tile([P, 256], U8, name="xc%d%d" % (m, gp), align_bytes=64) for gp in range(2)] for m in range(4)]
+        tab = const.tile([P, TOKEN_TILES, 2, P], BF16, name="tab")
+        zrow = const.tile([P, P], BF16, name="zrow")
+        zswp = const.tile([P, P], BF16, name="zswp")
+        lz = const.tile([P, 6, P], BF16, name="lz")
+        zt32 = const.tile([P, 2, 32], F32, name="zt32")
+        e01 = const.tile([P, 2, HALF], BF16, name="e01")
+        rmat = [const.tile([P, 4, 2, HALF], BF16, name="rmat%d" % c) for c in range(5)]
+        bvb = const.tile([P, 512], F32, name="bvb")
+        ident_f = const.tile([P, P], F32, name="ident_f")
+        ident_b = const.tile([P, P], BF16, name="ident_b")
+        warm_in = const.tile([P, 1], F32, name="warm_in")
+        warm_out = const.tile([P, 1], F32, name="warm_out")
+        zeros = const.tile([P, 512], BF16, name="zeros")
+
+        nc.vector.memset(zrow[:], 0.0)
+        nc.vector.memset(warm_in[:], 0.0)
+        nc.vector.memset(zeros[:], 0.0)
+        nc.vector.memset(planes[0][:].bitcast(I32), 0)
+        nc.vector.memset(planes[1][:].bitcast(I32), 0)
+        nc.vector.memset(planes[2][:].bitcast(I32), 0)
+        make_identity(nc, ident_f[:])
+        make_identity(nc, ident_b[:])
+
+        def load_plane(i):
+            for q in range(4):
+                nc.sync.dma_start(
+                    out=planes[i][32 * q : 32 * q + 4, :, :].bitcast(I32),
+                    in_=plane_src[i][:, 4 * q : 4 * q + 4, :].rearrange("g r n -> r g n").bitcast(I32),
+                )
+
+        def load_w(c):
+            src = Wq_words[:, :, 1024 * c : 1024 * (c + 1)] if c < 4 else Wkv_words[:, :, 1024 * (c - 4) : 1024 * (c - 3)]
+            nc.sync.dma_start(out=w[c][:].bitcast(I32), in_=src.rearrange("g p b -> p g b").bitcast(I32))
+
+        def load_x(m):
+            nc.sync.dma_start(out=xs[m][:], in_=x[0, P * m : P * (m + 1), :])
+
+        load_x(0)
+        nc.scalar.dma_start(out=tab[:, :, 0, HALF:P], in_=cos.rearrange("(m p) j -> p m j", p=P))
+        nc.scalar.dma_start(out=tab[:, :, 1, 0:HALF], in_=sin.rearrange("(m p) j -> p m j", p=P))
+        nc.scalar.copy(out=warm_out[:], in_=warm_in[:])
+        nc.sync.dma_start(out=zrow[0:16, :], in_=bq.rearrange("(h f) -> h f", f=P))
+        nc.sync.dma_start(out=zrow[16:24, :], in_=bkv.rearrange("(h f) -> h f", f=P))
+        load_x(1)
+        load_w(0)
+        load_plane(0)
+        load_x(2)
+        load_x(3)
+        load_plane(1)
+        load_w(1)
+        load_plane(2)
+        for c in range(2, 6):
+            load_w(c)
+
+        if WARM_MATMULS:
+            warm_ps = auxp.tile([P, 512], F32, name="warm_ps", tag="aux")
+            for r in range(WARM_MATMULS):
+                nc.tensor.matmul(out=warm_ps[:], lhsT=zeros[:, 0:P], rhs=zeros[:], start=True, stop=True)
+
+        def xprep(m):
+            for gp in range(2):
+                words = xs[m][:, 1024 * gp : 1024 * (gp + 1)].bitcast(F32)
+                xt = auxp.tile([P, 2, 2, P], F32, name="xt", tag="aux")
+                for gl in range(2):
+                    for u in range(2):
+                        nc.tensor.transpose(xt[:, gl, u, :], words[:, 256 * gl + u : 256 * (gl + 1) : 2], ident_f[:])
+                nc.scalar.copy(
+                    out=grouped[m][gp][:].bitcast(F32).rearrange("p (g r u) -> p g r u", g=2, u=2),
+                    in_=xt[:].rearrange("p g u r -> p g r u"),
+                )
+                nc.vector.quantize_mx(
+                    out=xq[m][gp][:].bitcast(E5M2X4), scales=xsc[m][gp][:], in_=grouped[m][gp][:]
+                )
+
+        def build_rmat_vector(c):
+            for a in range(2):
+                nc.vector.tensor_tensor(
+                    out=rmat[c][:, :, a, :],
+                    in0=e01[:, a : a + 1, :].to_broadcast([P, 4, HALF]),
+                    in1=lz[:, a, 4 * c : 4 * c + 4].unsqueeze(2).to_broadcast([P, 4, HALF]),
+                    op=ALU.mult,
+                )
+
+        def build_rmat_scalar(c):
+            for h in range(4):
+                for a in range(2):
+                    nc.scalar.activation(
+                        out=rmat[c][:, h, a, :], in_=e01[:, a, :], func=ACT.Copy, scale=zt32[:, a, 4 * c + h : 4 * c + h + 1]
+                    )
+
+        def out_view(c, m):
+            rows = slice(P * m, P * (m + 1))
+            if c < 4:
+                dst = out_0[0, 4 * c : 4 * c + 4, rows, :]
+            elif c == 4:
+                dst = out_1[0, :, rows, :]
+            else:
+                dst = out_2[0, :, rows, :]
+            return dst.rearrange("h p d -> p h d")
+
+        def halves(ap):
+            return ap.rearrange("p (h a j) -> p h a j", a=2, j=HALF)
+
+        def heads(ap):
+            return ap.rearrange("p (h f) -> p h f", f=P)
+
+        def first_stage(c, m):
+            acc = accp.tile([P, 512], F32, name="acc", tag="acc")
+            pl, off = plane_of[c]
+            for g in range(PASSES):
+                gp, gl = divmod(g, 2)
+                nc.tensor.matmul_mx(
+                    out=acc[:],
+                    lhsT=xq[m][gp][:, P * gl : P * (gl + 1)].bitcast(E5M2X4),
+                    lhsT_scale=xsc[m][gp][:, P * gl : P * (gl + 1)],
+                    rhs=w[c][:, g, :].bitcast(E2M1X4),
+                    rhs_scale=planes[pl][:, g, off : off + 512],
+                    start=(g == 0),
+                    stop=(g == PASSES - 1),
+                )
+            if c == 5:
+                o = work.tile([P, 512], F32, name="o", tag="o")
+                nc.vector.tensor_tensor(out=o[:], in0=acc[:], in1=bvb[:], op=ALU.add)
+                nc.sync.dma_start(out=out_view(c, m), in_=heads(o[:]))
+                return None
+            prod = work.tile([P, 2, 512], F32, name="prod", tag="prod")
+            nc.vector.tensor_tensor(
+                out=prod[:].rearrange("p t (h f) -> p t h f", f=P),
+                in0=heads(acc[:]).unsqueeze(1).to_broadcast([P, 2, 4, P]),
+                in1=tab[:, m, :, :].unsqueeze(2).to_broadcast([P, 2, 4, P]),
+                op=ALU.mult,
+            )
+            return prod
+
+        def second_stage(i, c, m, prod):
+            rb = auxp.tile([P, 512], F32, name="rb", tag="aux")
+            nc.tensor.matmul(
+                out=rb[:],
+                lhsT=lz[:, 2 + m, :],
+                rhs=rmat[c][:].rearrange("p h a j -> p (h a j)"),
+                start=True,
+                stop=True,
+            )
+            tb = work.tile([P, 512], F32, name="tb", tag="tb")
+            o = work.tile([P, 512], F32, name="o", tag="o")
+            if i in GPSIMD_BANKS:
+                rbs = work.tile([P, 512], F32, name="rbs", tag="rbs")
+                nc.scalar.copy(out=rbs[:], in_=rb[:])
+                nc.gpsimd.tensor_tensor(out=tb[:], in0=prod[:, 0, :], in1=rbs[:], op=ALU.add)
+            else:
+                nc.vector.tensor_tensor(out=tb[:], in0=prod[:, 0, :], in1=rb[:], op=ALU.add)
+            nc.gpsimd.tensor_tensor(
+                out=halves(o[:]), in0=halves(tb[:]), in1=halves(prod[:, 1, :])[:, :, ::-1, :], op=ALU.add
+            )
+            nc.sync.dma_start(out=out_view(c, m), in_=heads(o[:]))
+
+        nc.vector.tensor_tensor(out=e01[:, 0, :], in0=ident_b[:, 0:HALF], in1=ident_b[:, HALF:P], op=ALU.subtract)
+        nc.vector.tensor_tensor(out=e01[:, 1, :], in0=ident_b[:, 0:HALF], in1=ident_b[:, HALF:P], op=ALU.add)
+        nc.vector.tensor_copy(out=tab[:, :, 0, 0:HALF], in_=tab[:, :, 0, HALF:P])
+        nc.vector.tensor_scalar(out=tab[:, :, 1, HALF:P], in0=tab[:, :, 1, 0:HALF], scalar1=-1.0, scalar2=None, op0=ALU.mult)
+
+        nc.vector.tensor_copy(out=zswp[:, 0:HALF], in_=zrow[:, HALF:P])
+        nc.vector.tensor_copy(out=zswp[:, HALF:P], in_=zrow[:, 0:HALF])
+        xprep(0)
+        banks = [(c, m) for c in range(6) for m in range(TOKEN_TILES)]
+
+        misc = auxp.tile([P, 6, P], BF16, name="misc", tag="aux")
+        nc.tensor.transpose(misc[:, 0, :], zrow[:], ident_b[:])
+        nc.tensor.transpose(misc[:, 1, :], zswp[:], ident_b[:])
+        for m in range(TOKEN_TILES):
+            nc.tensor.transpose(misc[:, 2 + m, :], tab[:, m, :, :].rearrange("p t f -> p (t f)")[:, HALF : HALF + P], ident_b[:])
+        nc.vector.tensor_copy(out=lz[:], in_=misc[:])
+        nc.vector.tensor_copy(out=zt32[:], in_=misc[:, 0:2, 0:32])
+        build_rmat_vector(0)
+        xprep(1)
+        prods = {0: first_stage(0, 0)}
+        xprep(2)
+
+        for i in range(1, len(banks) + 1):
+            if i < len(banks):
+                c, m = banks[i]
+                prods[i] = first_stage(c, m)
+            pc, pm = banks[i - 1]
+            if prods[i - 1] is not None:
+                second_stage(i - 1, pc, pm, prods[i - 1])
+            if i == 1:
+                xprep(3)
+            if i % 4 == 1 and i < 17:
+                build_rmat_scalar(i // 4 + 1)
+            if i == 5:
+                bvp = auxp.tile([P, 512], F32, name="bvp", tag="aux")
+                for hv in range(4):
+                    nc.tensor.matmul(
+                        out=bvp[:, P * hv : P * (hv + 1)],
+                        lhsT=lz[:, 0, 20 + hv : 21 + hv].to_broadcast([P, P]),
+                        rhs=ident_b[:],
+                        start=True,
+                        stop=True,
+                    )
+                nc.scalar.copy(out=bvb[:], in_=bvp[:])

@@ -17,7 +17,6 @@ P = 128
 PASSES = 4
 TOKEN_TILES = 4
 HALF = 64
-GPSIMD_BANKS = (3, 8, 13, 18)
 WARM_MATMULS = 6
 
 FLOPS = 2 * 512 * 2048 * 3072
@@ -30,8 +29,8 @@ def tile_qwen2attention_pa_kernel(
     with ExitStack() as ctx:
         const = ctx.enter_context(tc.tile_pool(name="const", bufs=1))
         work = ctx.enter_context(tc.tile_pool(name="work", bufs=4))
-        accp = ctx.enter_context(tc.psum_pool(name="accp", bufs=4))
-        auxp = ctx.enter_context(tc.psum_pool(name="auxp", bufs=4))
+        accp = ctx.enter_context(tc.psum_pool(name="accp", bufs=3))
+        auxp = ctx.enter_context(tc.psum_pool(name="auxp", bufs=5))
 
         plane_cols = (512, 1536, 1024)
         planes = [
@@ -45,8 +44,8 @@ def tile_qwen2attention_pa_kernel(
             [const.tile([P, 1024], BF16, name="xg%d%d" % (m, gp), align_bytes=64) for gp in range(2)]
             for m in range(4)
         ]
-        xq = [[const.tile([P, 256], U32, name="xq%d%d" % (m, gp), align_bytes=64) for gp in range(2)] for m in range(4)]
-        xsc = [[const.tile([P, 256], U8, name="xc%d%d" % (m, gp), align_bytes=64) for gp in range(2)] for m in range(4)]
+        xq = [const.tile([P, 512], U32, name="xq%d" % g, align_bytes=64) for g in range(PASSES)]
+        xsc = [const.tile([P, 512], U8, name="xc%d" % g, align_bytes=64) for g in range(PASSES)]
         tab = const.tile([P, TOKEN_TILES, 2, P], BF16, name="tab")
         zrow = const.tile([P, P], BF16, name="zrow")
         zswp = const.tile([P, P], BF16, name="zswp")
@@ -87,7 +86,7 @@ def tile_qwen2attention_pa_kernel(
         load_x(0)
         nc.scalar.dma_start(out=tab[:, :, 0, HALF:P], in_=cos.rearrange("(m p) j -> p m j", p=P))
         nc.scalar.dma_start(out=tab[:, :, 1, 0:HALF], in_=sin.rearrange("(m p) j -> p m j", p=P))
-        nc.scalar.copy(out=warm_out[:], in_=warm_in[:])
+        nc.scalar.activation(out=warm_out[:], in_=warm_in[:], func=ACT.Identity, bias=warm_in[:], scale=1.0)
         nc.sync.dma_start(out=zrow[0:16, :], in_=bq.rearrange("(h f) -> h f", f=P))
         nc.sync.dma_start(out=zrow[16:24, :], in_=bkv.rearrange("(h f) -> h f", f=P))
         load_x(1)
@@ -96,17 +95,16 @@ def tile_qwen2attention_pa_kernel(
         load_x(2)
         load_x(3)
         load_plane(1)
-        load_w(1)
-        load_plane(2)
-        for c in range(2, 6):
+        for c in (2, 1, 3, 4, 5):
+            if c == 4:
+                load_plane(2)
             load_w(c)
 
-        if WARM_MATMULS:
-            warm_ps = auxp.tile([P, 512], F32, name="warm_ps", tag="aux")
-            for r in range(WARM_MATMULS):
-                nc.tensor.matmul(out=warm_ps[:], lhsT=zeros[:, 0:P], rhs=zeros[:], start=True, stop=True)
+        warm_ps = auxp.tile([P, 512], F32, name="warm_ps", tag="aux")
+        for r in range(WARM_MATMULS):
+            nc.tensor.matmul(out=warm_ps[:], lhsT=zeros[:, 0:P], rhs=zeros[:], start=True, stop=True)
 
-        def xprep(m):
+        def x_transpose(m):
             for gp in range(2):
                 words = xs[m][:, 1024 * gp : 1024 * (gp + 1)].bitcast(F32)
                 xt = auxp.tile([P, 2, 2, P], F32, name="xt", tag="aux")
@@ -117,8 +115,14 @@ def tile_qwen2attention_pa_kernel(
                     out=grouped[m][gp][:].bitcast(F32).rearrange("p (g r u) -> p g r u", g=2, u=2),
                     in_=xt[:].rearrange("p g u r -> p g r u"),
                 )
+
+        def x_quantize(m):
+            for g in range(PASSES):
+                gp, gl = divmod(g, 2)
                 nc.vector.quantize_mx(
-                    out=xq[m][gp][:].bitcast(E5M2X4), scales=xsc[m][gp][:], in_=grouped[m][gp][:]
+                    out=xq[g][:, P * m : P * (m + 1)].bitcast(E5M2X4),
+                    scales=xsc[g][:, P * m : P * (m + 1)],
+                    in_=grouped[m][gp][:, 512 * gl : 512 * (gl + 1)],
                 )
 
         def build_rmat_vector(c):
@@ -137,81 +141,115 @@ def tile_qwen2attention_pa_kernel(
                         out=rmat[c][:, h, a, :], in_=e01[:, a, :], func=ACT.Copy, scale=zt32[:, a, 4 * c + h : 4 * c + h + 1]
                     )
 
-        def out_view(c, m):
-            rows = slice(P * m, P * (m + 1))
-            if c < 4:
-                dst = out_0[0, 4 * c : 4 * c + 4, rows, :]
-            elif c == 4:
-                dst = out_1[0, :, rows, :]
-            else:
-                dst = out_2[0, :, rows, :]
-            return dst.rearrange("h p d -> p h d")
-
         def halves(ap):
             return ap.rearrange("p (h a j) -> p h a j", a=2, j=HALF)
 
-        def heads(ap):
+        def quarters(ap):
             return ap.rearrange("p (h f) -> p h f", f=P)
 
-        def first_stage(c, m):
+        def out_view(unit):
+            kind, c, k = unit
+            if kind == "T":
+                rows = slice(P * k, P * (k + 1))
+                if c < 4:
+                    dst = out_0[0, 4 * c : 4 * c + 4, rows, :]
+                elif c == 4:
+                    dst = out_1[0, :, rows, :]
+                else:
+                    dst = out_2[0, :, rows, :]
+                return dst.rearrange("h p d -> p h d")
+            dst = out_0[0, 4 * c + k, :, :] if c < 4 else out_1[0, k, :, :]
+            return dst.rearrange("(m p) d -> p m d", p=P)
+
+        def multiply(unit):
+            kind, c, k = unit
             acc = accp.tile([P, 512], F32, name="acc", tag="acc")
             pl, off = plane_of[c]
             for g in range(PASSES):
-                gp, gl = divmod(g, 2)
-                nc.tensor.matmul_mx(
-                    out=acc[:],
-                    lhsT=xq[m][gp][:, P * gl : P * (gl + 1)].bitcast(E5M2X4),
-                    lhsT_scale=xsc[m][gp][:, P * gl : P * (gl + 1)],
-                    rhs=w[c][:, g, :].bitcast(E2M1X4),
-                    rhs_scale=planes[pl][:, g, off : off + 512],
-                    start=(g == 0),
-                    stop=(g == PASSES - 1),
+                if kind == "T":
+                    nc.tensor.matmul_mx(
+                        out=acc[:],
+                        lhsT=xq[g][:, P * k : P * (k + 1)].bitcast(E5M2X4),
+                        lhsT_scale=xsc[g][:, P * k : P * (k + 1)],
+                        rhs=w[c][:, g, :].bitcast(E2M1X4),
+                        rhs_scale=planes[pl][:, g, off : off + 512],
+                        start=(g == 0),
+                        stop=(g == PASSES - 1),
+                    )
+                else:
+                    nc.tensor.matmul_mx(
+                        out=acc[:],
+                        lhsT=w[c][:, g, 256 * k : 256 * (k + 1)].bitcast(E2M1X4),
+                        lhsT_scale=planes[pl][:, g, off + P * k : off + P * (k + 1)],
+                        rhs=xq[g][:].bitcast(E5M2X4),
+                        rhs_scale=xsc[g][:],
+                        start=(g == 0),
+                        stop=(g == PASSES - 1),
+                    )
+            if kind == "F":
+                biased = work.tile([P, 512], F32, name="biased", tag="biased")
+                nc.scalar.activation(
+                    out=biased[:], in_=acc[:], func=ACT.Identity, bias=zt32[:, 0, 4 * c + k : 4 * c + k + 1], scale=1.0
                 )
+                return biased
+            return acc
+
+        def products(unit, src):
+            kind, c, k = unit
             if c == 5:
                 o = work.tile([P, 512], F32, name="o", tag="o")
-                nc.vector.tensor_tensor(out=o[:], in0=acc[:], in1=bvb[:], op=ALU.add)
-                nc.sync.dma_start(out=out_view(c, m), in_=heads(o[:]))
+                nc.vector.tensor_tensor(out=o[:], in0=src[:], in1=bvb[:], op=ALU.add)
+                nc.sync.dma_start(out=out_view(unit), in_=quarters(o[:]))
                 return None
             prod = work.tile([P, 2, 512], F32, name="prod", tag="prod")
-            nc.vector.tensor_tensor(
-                out=prod[:].rearrange("p t (h f) -> p t h f", f=P),
-                in0=heads(acc[:]).unsqueeze(1).to_broadcast([P, 2, 4, P]),
-                in1=tab[:, m, :, :].unsqueeze(2).to_broadcast([P, 2, 4, P]),
-                op=ALU.mult,
-            )
+            if kind == "T":
+                nc.vector.tensor_tensor(
+                    out=prod[:].rearrange("p t (h f) -> p t h f", f=P),
+                    in0=quarters(src[:]).unsqueeze(1).to_broadcast([P, 2, 4, P]),
+                    in1=tab[:, k, :, :].unsqueeze(2).to_broadcast([P, 2, 4, P]),
+                    op=ALU.mult,
+                )
+            else:
+                back = auxp.tile([P, 512], F32, name="back", tag="aux")
+                for m in range(TOKEN_TILES):
+                    nc.tensor.transpose(back[:, P * m : P * (m + 1)], src[:, P * m : P * (m + 1)], ident_f[:])
+                nc.vector.tensor_tensor(
+                    out=prod[:].rearrange("p t (m f) -> p t m f", f=P),
+                    in0=quarters(back[:]).unsqueeze(1).to_broadcast([P, 2, 4, P]),
+                    in1=tab[:].rearrange("p m t f -> p t m f"),
+                    op=ALU.mult,
+                )
             return prod
 
-        def second_stage(i, c, m, prod):
-            rb = auxp.tile([P, 512], F32, name="rb", tag="aux")
-            nc.tensor.matmul(
-                out=rb[:],
-                lhsT=lz[:, 2 + m, :],
-                rhs=rmat[c][:].rearrange("p h a j -> p (h a j)"),
-                start=True,
-                stop=True,
-            )
-            tb = work.tile([P, 512], F32, name="tb", tag="tb")
+        def finish(unit, prod):
+            kind, c, k = unit
             o = work.tile([P, 512], F32, name="o", tag="o")
-            if i in GPSIMD_BANKS:
-                rbs = work.tile([P, 512], F32, name="rbs", tag="rbs")
-                nc.scalar.copy(out=rbs[:], in_=rb[:])
-                nc.gpsimd.tensor_tensor(out=tb[:], in0=prod[:, 0, :], in1=rbs[:], op=ALU.add)
-            else:
-                nc.vector.tensor_tensor(out=tb[:], in0=prod[:, 0, :], in1=rb[:], op=ALU.add)
+            first = prod[:, 0, :]
+            if kind == "T":
+                rb = auxp.tile([P, 512], F32, name="rb", tag="aux")
+                nc.tensor.matmul(
+                    out=rb[:],
+                    lhsT=lz[:, 2 + k, :],
+                    rhs=rmat[c][:].rearrange("p h a j -> p (h a j)"),
+                    start=True,
+                    stop=True,
+                )
+                tb = work.tile([P, 512], F32, name="tb", tag="tb")
+                nc.vector.tensor_tensor(out=tb[:], in0=first, in1=rb[:], op=ALU.add)
+                first = tb[:]
             nc.gpsimd.tensor_tensor(
-                out=halves(o[:]), in0=halves(tb[:]), in1=halves(prod[:, 1, :])[:, :, ::-1, :], op=ALU.add
+                out=halves(o[:]), in0=halves(first), in1=halves(prod[:, 1, :])[:, :, ::-1, :], op=ALU.add
             )
-            nc.sync.dma_start(out=out_view(c, m), in_=heads(o[:]))
+            nc.sync.dma_start(out=out_view(unit), in_=quarters(o[:]))
 
         nc.vector.tensor_tensor(out=e01[:, 0, :], in0=ident_b[:, 0:HALF], in1=ident_b[:, HALF:P], op=ALU.subtract)
         nc.vector.tensor_tensor(out=e01[:, 1, :], in0=ident_b[:, 0:HALF], in1=ident_b[:, HALF:P], op=ALU.add)
         nc.vector.tensor_copy(out=tab[:, :, 0, 0:HALF], in_=tab[:, :, 0, HALF:P])
         nc.vector.tensor_scalar(out=tab[:, :, 1, HALF:P], in0=tab[:, :, 1, 0:HALF], scalar1=-1.0, scalar2=None, op0=ALU.mult)
-
         nc.vector.tensor_copy(out=zswp[:, 0:HALF], in_=zrow[:, HALF:P])
         nc.vector.tensor_copy(out=zswp[:, HALF:P], in_=zrow[:, 0:HALF])
-        xprep(0)
-        banks = [(c, m) for c in range(6) for m in range(TOKEN_TILES)]
+        x_transpose(0)
+        x_quantize(0)
 
         misc = auxp.tile([P, 6, P], BF16, name="misc", tag="aux")
         nc.tensor.transpose(misc[:, 0, :], zrow[:], ident_b[:])
@@ -221,21 +259,28 @@ def tile_qwen2attention_pa_kernel(
         nc.vector.tensor_copy(out=lz[:], in_=misc[:])
         nc.vector.tensor_copy(out=zt32[:], in_=misc[:, 0:2, 0:32])
         build_rmat_vector(0)
-        xprep(1)
-        prods = {0: first_stage(0, 0)}
-        xprep(2)
+        x_transpose(1)
+        x_quantize(1)
 
-        for i in range(1, len(banks) + 1):
-            if i < len(banks):
-                c, m = banks[i]
-                prods[i] = first_stage(c, m)
-            pc, pm = banks[i - 1]
-            if prods[i - 1] is not None:
-                second_stage(i - 1, pc, pm, prods[i - 1])
-            if i == 1:
-                xprep(3)
-            if i % 4 == 1 and i < 17:
-                build_rmat_scalar(i // 4 + 1)
+        units = [("T", 0, 0), ("T", 0, 1), ("T", 0, 2), ("T", 0, 3), ("F", 2, 0), ("T", 1, 0), ("F", 2, 1), ("T", 1, 1), ("F", 2, 2), ("T", 1, 2), ("F", 2, 3), ("T", 1, 3), ("F", 3, 0), ("T", 4, 0), ("F", 3, 1), ("T", 4, 1), ("F", 3, 2), ("T", 4, 2), ("F", 3, 3), ("T", 4, 3), ("T", 5, 0), ("T", 5, 1), ("T", 5, 2), ("T", 5, 3)]
+        n = len(units)
+        srcs = {}
+        prods = {}
+        for i in range(n + 2):
+            if i in (2, 3):
+                prods[i - 1] = products(units[i - 1], srcs[i - 1])
+                x_quantize(i)
+            if i < n:
+                srcs[i] = multiply(units[i])
+            if i in (0, 1):
+                x_transpose(i + 2)
+            if 1 <= i <= n and (i - 1) not in prods:
+                prods[i - 1] = products(units[i - 1], srcs[i - 1])
+            if i >= 2 and prods[i - 2] is not None:
+                finish(units[i - 2], prods[i - 2])
+            if i == 3:
+                for c in (1, 4):
+                    build_rmat_scalar(c)
             if i == 5:
                 bvp = auxp.tile([P, 512], F32, name="bvp", tag="aux")
                 for hv in range(4):

@@ -18,6 +18,7 @@ PASSES = 4
 TOKEN_TILES = 4
 HALF = 64
 WARM_MATMULS = 6
+ROUND = 2
 
 FLOPS = 2 * 512 * 2048 * 3072
 
@@ -28,9 +29,9 @@ def tile_qwen2attention_pa_kernel(
     nc = tc.nc
     with ExitStack() as ctx:
         const = ctx.enter_context(tc.tile_pool(name="const", bufs=1))
-        work = ctx.enter_context(tc.tile_pool(name="work", bufs=4))
-        accp = ctx.enter_context(tc.psum_pool(name="accp", bufs=3))
-        auxp = ctx.enter_context(tc.psum_pool(name="auxp", bufs=5))
+        work = ctx.enter_context(tc.tile_pool(name="work", bufs=3))
+        accp = ctx.enter_context(tc.psum_pool(name="accp", bufs=4))
+        auxp = ctx.enter_context(tc.psum_pool(name="auxp", bufs=4))
 
         plane_cols = (512, 1536, 1024)
         planes = [
@@ -52,7 +53,7 @@ def tile_qwen2attention_pa_kernel(
         lz = const.tile([P, 6, P], BF16, name="lz")
         zt32 = const.tile([P, 2, 32], F32, name="zt32")
         e01 = const.tile([P, 2, HALF], BF16, name="e01")
-        rmat = [const.tile([P, 4, 2, HALF], BF16, name="rmat%d" % c) for c in range(5)]
+        rmat = {0: const.tile([P, 4, 2, HALF], BF16, name="rmat0")}
         bvb = const.tile([P, 512], F32, name="bvb")
         ident_f = const.tile([P, P], F32, name="ident_f")
         ident_b = const.tile([P, P], BF16, name="ident_b")
@@ -60,10 +61,10 @@ def tile_qwen2attention_pa_kernel(
         warm_out = const.tile([P, 1], F32, name="warm_out")
         zeros = const.tile([P, 512], BF16, name="zeros")
 
-        nc.vector.memset(zrow[:], 0.0)
+        nc.vector.memset(planes[0][:].bitcast(I32), 0)
         nc.vector.memset(warm_in[:], 0.0)
         nc.vector.memset(zeros[:], 0.0)
-        nc.vector.memset(planes[0][:].bitcast(I32), 0)
+        nc.vector.memset(zrow[:], 0.0)
         nc.vector.memset(planes[1][:].bitcast(I32), 0)
         nc.vector.memset(planes[2][:].bitcast(I32), 0)
         make_identity(nc, ident_f[:])
@@ -80,25 +81,27 @@ def tile_qwen2attention_pa_kernel(
             src = Wq_words[:, :, 1024 * c : 1024 * (c + 1)] if c < 4 else Wkv_words[:, :, 1024 * (c - 4) : 1024 * (c - 3)]
             nc.sync.dma_start(out=w[c][:].bitcast(I32), in_=src.rearrange("g p b -> p g b").bitcast(I32))
 
-        def load_x(m):
-            nc.sync.dma_start(out=xs[m][:], in_=x[0, P * m : P * (m + 1), :])
+        def load_x(queue, m):
+            queue.dma_start(out=xs[m][:], in_=x[0, P * m : P * (m + 1), :])
 
-        load_x(0)
+        load_x(nc.scalar, 0)
+        load_x(nc.scalar, 1)
         nc.scalar.dma_start(out=tab[:, :, 0, HALF:P], in_=cos.rearrange("(m p) j -> p m j", p=P))
-        nc.scalar.dma_start(out=tab[:, :, 1, 0:HALF], in_=sin.rearrange("(m p) j -> p m j", p=P))
         nc.scalar.activation(out=warm_out[:], in_=warm_in[:], func=ACT.Identity, bias=warm_in[:], scale=1.0)
+        load_plane(0)
+        load_w(0)
+        nc.sync.dma_start(out=tab[:, :, 1, 0:HALF], in_=sin.rearrange("(m p) j -> p m j", p=P))
         nc.sync.dma_start(out=zrow[0:16, :], in_=bq.rearrange("(h f) -> h f", f=P))
         nc.sync.dma_start(out=zrow[16:24, :], in_=bkv.rearrange("(h f) -> h f", f=P))
-        load_x(1)
-        load_w(0)
-        load_plane(0)
-        load_x(2)
-        load_x(3)
+        load_x(nc.sync, 2)
+        load_x(nc.sync, 3)
         load_plane(1)
-        for c in (2, 1, 3, 4, 5):
-            if c == 4:
-                load_plane(2)
-            load_w(c)
+        load_w(1)
+        load_w(2)
+        load_w(3)
+        load_plane(2)
+        load_w(4)
+        load_w(5)
 
         warm_ps = auxp.tile([P, 512], F32, name="warm_ps", tag="aux")
         for r in range(WARM_MATMULS):
@@ -133,16 +136,6 @@ def tile_qwen2attention_pa_kernel(
                     in1=lz[:, a, 4 * c : 4 * c + 4].unsqueeze(2).to_broadcast([P, 4, HALF]),
                     op=ALU.mult,
                 )
-
-        def build_rmat_scalar(c):
-            for h in range(4):
-                for a in range(2):
-                    nc.scalar.activation(
-                        out=rmat[c][:, h, a, :], in_=e01[:, a, :], func=ACT.Copy, scale=zt32[:, a, 4 * c + h : 4 * c + h + 1]
-                    )
-
-        def halves(ap):
-            return ap.rearrange("p (h a j) -> p h a j", a=2, j=HALF)
 
         def quarters(ap):
             return ap.rearrange("p (h f) -> p h f", f=P)
@@ -187,69 +180,72 @@ def tile_qwen2attention_pa_kernel(
                         stop=(g == PASSES - 1),
                     )
             if kind == "F":
-                biased = work.tile([P, 512], F32, name="biased", tag="biased")
+                biased = work.tile([P, 512], F32, name="biased", tag="biased", bufs=6)
                 nc.scalar.activation(
                     out=biased[:], in_=acc[:], func=ACT.Identity, bias=zt32[:, 0, 4 * c + k : 4 * c + k + 1], scale=1.0
                 )
                 return biased
             return acc
 
-        def products(unit, src):
-            kind, c, k = unit
-            if c == 5:
-                o = work.tile([P, 512], F32, name="o", tag="o")
-                nc.vector.tensor_tensor(out=o[:], in0=src[:], in1=bvb[:], op=ALU.add)
-                nc.sync.dma_start(out=out_view(unit), in_=quarters(o[:]))
-                return None
-            prod = work.tile([P, 2, 512], F32, name="prod", tag="prod")
-            if kind == "T":
+        def products(rnd, srcs):
+            ins = []
+            for unit, src in zip(rnd, srcs):
+                if unit[0] == "F":
+                    back = auxp.tile([P, 512], F32, name="back", tag="aux")
+                    for m in range(TOKEN_TILES):
+                        nc.tensor.transpose(back[:, P * m : P * (m + 1)], src[:, P * m : P * (m + 1)], ident_f[:])
+                    ins.append(back)
+                else:
+                    ins.append(src)
+            prod = work.tile([P, 2, len(rnd), 512], F32, name="prod", tag="prod")
+            for j, unit in enumerate(rnd):
+                if unit[0] == "T":
+                    table = tab[:, unit[2], :, :].unsqueeze(2).to_broadcast([P, 2, 4, P])
+                else:
+                    table = tab[:].rearrange("p m t f -> p t m f")
                 nc.vector.tensor_tensor(
-                    out=prod[:].rearrange("p t (h f) -> p t h f", f=P),
-                    in0=quarters(src[:]).unsqueeze(1).to_broadcast([P, 2, 4, P]),
-                    in1=tab[:, k, :, :].unsqueeze(2).to_broadcast([P, 2, 4, P]),
-                    op=ALU.mult,
-                )
-            else:
-                back = auxp.tile([P, 512], F32, name="back", tag="aux")
-                for m in range(TOKEN_TILES):
-                    nc.tensor.transpose(back[:, P * m : P * (m + 1)], src[:, P * m : P * (m + 1)], ident_f[:])
-                nc.vector.tensor_tensor(
-                    out=prod[:].rearrange("p t (m f) -> p t m f", f=P),
-                    in0=quarters(back[:]).unsqueeze(1).to_broadcast([P, 2, 4, P]),
-                    in1=tab[:].rearrange("p m t f -> p t m f"),
+                    out=prod[:, :, j, :].rearrange("p t (h f) -> p t h f", f=P),
+                    in0=quarters(ins[j][:]).unsqueeze(1).to_broadcast([P, 2, 4, P]),
+                    in1=table,
                     op=ALU.mult,
                 )
             return prod
 
-        def finish(unit, prod):
-            kind, c, k = unit
-            o = work.tile([P, 512], F32, name="o", tag="o")
-            first = prod[:, 0, :]
-            if kind == "T":
-                rb = auxp.tile([P, 512], F32, name="rb", tag="aux")
-                nc.tensor.matmul(
-                    out=rb[:],
-                    lhsT=lz[:, 2 + k, :],
-                    rhs=rmat[c][:].rearrange("p h a j -> p (h a j)"),
-                    start=True,
-                    stop=True,
+        def finish(rnd, prod, span):
+            o = work.tile([P, len(rnd), 512], F32, name="o", tag="o")
+            for j, unit in enumerate(rnd):
+                kind, c, k = unit
+                if kind == "T":
+                    rb = auxp.tile([P, 512], F32, name="rb", tag="aux")
+                    nc.tensor.matmul(
+                        out=rb[:],
+                        lhsT=lz[:, 2 + k, :],
+                        rhs=rmat[c][:].rearrange("p h a j -> p (h a j)"),
+                        start=True,
+                        stop=True,
+                    )
+                    nc.vector.tensor_tensor(out=prod[:, 0, j, :], in0=prod[:, 0, j, :], in1=rb[:], op=ALU.add)
+            for j0 in range(0, len(rnd), span):
+                j1 = min(j0 + span, len(rnd))
+                nc.gpsimd.tensor_tensor(
+                    out=o[:, j0:j1, :].rearrange("p u (h a j) -> p (u h) a j", a=2, j=HALF),
+                    in0=prod[:, 0, j0:j1, :].rearrange("p u (h a j) -> p (u h) a j", a=2, j=HALF),
+                    in1=prod[:, 1, j0:j1, :].rearrange("p u (h a j) -> p (u h) a j", a=2, j=HALF)[:, :, ::-1, :],
+                    op=ALU.add,
                 )
-                tb = work.tile([P, 512], F32, name="tb", tag="tb")
-                nc.vector.tensor_tensor(out=tb[:], in0=first, in1=rb[:], op=ALU.add)
-                first = tb[:]
-            nc.gpsimd.tensor_tensor(
-                out=halves(o[:]), in0=halves(first), in1=halves(prod[:, 1, :])[:, :, ::-1, :], op=ALU.add
-            )
-            nc.sync.dma_start(out=out_view(unit), in_=quarters(o[:]))
+                for j in range(j0, j1):
+                    nc.sync.dma_start(out=out_view(rnd[j]), in_=quarters(o[:, j, :]))
 
         nc.vector.tensor_tensor(out=e01[:, 0, :], in0=ident_b[:, 0:HALF], in1=ident_b[:, HALF:P], op=ALU.subtract)
         nc.vector.tensor_tensor(out=e01[:, 1, :], in0=ident_b[:, 0:HALF], in1=ident_b[:, HALF:P], op=ALU.add)
+        x_transpose(0)
+        x_quantize(0)
         nc.vector.tensor_copy(out=tab[:, :, 0, 0:HALF], in_=tab[:, :, 0, HALF:P])
         nc.vector.tensor_scalar(out=tab[:, :, 1, HALF:P], in0=tab[:, :, 1, 0:HALF], scalar1=-1.0, scalar2=None, op0=ALU.mult)
         nc.vector.tensor_copy(out=zswp[:, 0:HALF], in_=zrow[:, HALF:P])
         nc.vector.tensor_copy(out=zswp[:, HALF:P], in_=zrow[:, 0:HALF])
-        x_transpose(0)
-        x_quantize(0)
+        x_transpose(1)
+        x_quantize(1)
 
         misc = auxp.tile([P, 6, P], BF16, name="misc", tag="aux")
         nc.tensor.transpose(misc[:, 0, :], zrow[:], ident_b[:])
@@ -259,36 +255,50 @@ def tile_qwen2attention_pa_kernel(
         nc.vector.tensor_copy(out=lz[:], in_=misc[:])
         nc.vector.tensor_copy(out=zt32[:], in_=misc[:, 0:2, 0:32])
         build_rmat_vector(0)
-        x_transpose(1)
-        x_quantize(1)
 
-        units = [("T", 0, 0), ("T", 0, 1), ("T", 0, 2), ("T", 0, 3), ("F", 2, 0), ("T", 1, 0), ("F", 2, 1), ("T", 1, 1), ("F", 2, 2), ("T", 1, 2), ("F", 2, 3), ("T", 1, 3), ("F", 3, 0), ("T", 4, 0), ("F", 3, 1), ("T", 4, 1), ("F", 3, 2), ("T", 4, 2), ("F", 3, 3), ("T", 4, 3), ("T", 5, 0), ("T", 5, 1), ("T", 5, 2), ("T", 5, 3)]
-        n = len(units)
-        srcs = {}
-        prods = {}
-        for i in range(n + 2):
-            if i in (2, 3):
-                prods[i - 1] = products(units[i - 1], srcs[i - 1])
-                x_quantize(i)
-            if i < n:
-                srcs[i] = multiply(units[i])
-            if i in (0, 1):
-                x_transpose(i + 2)
-            if 1 <= i <= n and (i - 1) not in prods:
-                prods[i - 1] = products(units[i - 1], srcs[i - 1])
-            if i >= 2 and prods[i - 2] is not None:
-                finish(units[i - 2], prods[i - 2])
-            if i == 3:
-                for c in (1, 4):
-                    build_rmat_scalar(c)
-            if i == 5:
-                bvp = auxp.tile([P, 512], F32, name="bvp", tag="aux")
-                for hv in range(4):
-                    nc.tensor.matmul(
-                        out=bvp[:, P * hv : P * (hv + 1)],
-                        lhsT=lz[:, 0, 20 + hv : 21 + hv].to_broadcast([P, P]),
-                        rhs=ident_b[:],
-                        start=True,
-                        stop=True,
-                    )
-                nc.scalar.copy(out=bvb[:], in_=bvp[:])
+        def value_heads(unit, src):
+            o = work.tile([P, 512], F32, name="ov", tag="ov")
+            nc.vector.tensor_tensor(out=o[:], in0=src[:], in1=bvb[:], op=ALU.add)
+            nc.sync.dma_start(out=out_view(unit), in_=quarters(o[:]))
+
+        first = [[("T", 0, m)] for m in range(TOKEN_TILES)]
+        s0 = [multiply(first[0][0])]
+        x_transpose(2)
+        s1 = [multiply(first[1][0])]
+        x_transpose(3)
+        p0 = products(first[0], s0)
+        p1 = products(first[1], s1)
+        x_quantize(2)
+        s2 = [multiply(first[2][0])]
+        finish(first[0], p0, 1)
+        p2 = products(first[2], s2)
+        x_quantize(3)
+        s3 = [multiply(first[3][0])]
+        finish(first[1], p1, 1)
+
+        heads = [("F", c, k) for c in (1, 2, 3, 4) for k in range(4)]
+        rounds = [heads[j : j + ROUND] for j in range(0, len(heads), ROUND)]
+        srcs = [[multiply(unit) for unit in rounds[0]]]
+        p3 = products(first[3], s3)
+        finish(first[2], p2, 1)
+        bvp = auxp.tile([P, 512], F32, name="bvp", tag="aux")
+        for hv in range(4):
+            nc.tensor.matmul(
+                out=bvp[:, P * hv : P * (hv + 1)],
+                lhsT=lz[:, 0, 20 + hv : 21 + hv].to_broadcast([P, P]),
+                rhs=ident_b[:],
+                start=True,
+                stop=True,
+            )
+        nc.scalar.copy(out=bvb[:], in_=bvp[:])
+        for r in range(1, len(rounds)):
+            srcs.append([multiply(unit) for unit in rounds[r]])
+            if r == 1:
+                finish(first[3], p3, 1)
+            finish(rounds[r - 1], products(rounds[r - 1], srcs[r - 1]), 2)
+        values = [("T", 5, m) for m in range(TOKEN_TILES)]
+        for unit in values[0:2]:
+            value_heads(unit, multiply(unit))
+        finish(rounds[-1], products(rounds[-1], srcs[-1]), 1)
+        for unit in values[2:4]:
+            value_heads(unit, multiply(unit))

@@ -32,6 +32,7 @@ def tile_qwen2attention_pa_kernel(
         work = ctx.enter_context(tc.tile_pool(name="work", bufs=3))
         accp = ctx.enter_context(tc.psum_pool(name="accp", bufs=4))
         auxp = ctx.enter_context(tc.psum_pool(name="auxp", bufs=4))
+        ctx.enter_context(tc.manual_schedule(engines={mybir.EngineType.PE}))
 
         plane_cols = (512, 1536, 1024)
         planes = [
@@ -84,7 +85,7 @@ def tile_qwen2attention_pa_kernel(
         def load_x(queue, m):
             queue.dma_start(out=xs[m][:], in_=x[0, P * m : P * (m + 1), :])
 
-        load_x(nc.scalar, 0)
+        load_x(nc.sync, 0)
         load_x(nc.scalar, 1)
         nc.scalar.dma_start(out=tab[:, :, 0, HALF:P], in_=cos.rearrange("(m p) j -> p m j", p=P))
         nc.scalar.activation(out=warm_out[:], in_=warm_in[:], func=ACT.Identity, bias=warm_in[:], scale=1.0)

@@ -17,7 +17,8 @@ P = 128
 PASSES = 4
 TOKEN_TILES = 4
 HALF = 64
-WARM_MATMULS = 6
+WARM_MATMULS = 5
+HOLD_MATMULS = 2
 ROUND = 2
 
 FLOPS = 2 * 512 * 2048 * 3072
@@ -62,9 +63,9 @@ def tile_qwen2attention_pa_kernel(
         warm_out = const.tile([P, 1], F32, name="warm_out")
         zeros = const.tile([P, 512], BF16, name="zeros")
 
+        nc.gpsimd.memset(zeros[:], 0.0)
         nc.vector.memset(planes[0][:].bitcast(I32), 0)
         nc.vector.memset(warm_in[:], 0.0)
-        nc.vector.memset(zeros[:], 0.0)
         nc.vector.memset(zrow[:], 0.0)
         nc.vector.memset(planes[1][:].bitcast(I32), 0)
         nc.vector.memset(planes[2][:].bitcast(I32), 0)
@@ -240,6 +241,9 @@ def tile_qwen2attention_pa_kernel(
         nc.vector.tensor_tensor(out=e01[:, 0, :], in0=ident_b[:, 0:HALF], in1=ident_b[:, HALF:P], op=ALU.subtract)
         nc.vector.tensor_tensor(out=e01[:, 1, :], in0=ident_b[:, 0:HALF], in1=ident_b[:, HALF:P], op=ALU.add)
         x_transpose(0)
+        hold_ps = accp.tile([P, 512], F32, name="hold_ps", tag="acc")
+        for r in range(HOLD_MATMULS):
+            nc.tensor.matmul(out=hold_ps[:], lhsT=zeros[:, 0:P], rhs=zeros[:], start=True, stop=True)
         x_quantize(0)
         nc.vector.tensor_copy(out=tab[:, :, 0, 0:HALF], in_=tab[:, :, 0, HALF:P])
         nc.vector.tensor_scalar(out=tab[:, :, 1, HALF:P], in0=tab[:, :, 1, 0:HALF], scalar1=-1.0, scalar2=None, op0=ALU.mult)
@@ -247,6 +251,7 @@ def tile_qwen2attention_pa_kernel(
         nc.vector.tensor_copy(out=zswp[:, HALF:P], in_=zrow[:, 0:HALF])
         x_transpose(1)
         x_quantize(1)
+        early = [multiply(("T", 0, 0))]
 
         misc = auxp.tile([P, 6, P], BF16, name="misc", tag="aux")
         nc.tensor.transpose(misc[:, 0, :], zrow[:], ident_b[:])
@@ -263,7 +268,7 @@ def tile_qwen2attention_pa_kernel(
             nc.sync.dma_start(out=out_view(unit), in_=quarters(o[:]))
 
         first = [[("T", 0, m)] for m in range(TOKEN_TILES)]
-        s0 = [multiply(first[0][0])]
+        s0 = early
         x_transpose(2)
         s1 = [multiply(first[1][0])]
         x_transpose(3)

@@ -19,7 +19,7 @@ TOKEN_TILES = 4
 HALF = 64
 WARM_MATMULS = 5
 HOLD_MATMULS = 2
-ROUND = 2
+ROUND_SIZES = (4, 4, 4, 2, 2)
 
 FLOPS = 2 * 512 * 2048 * 3072
 
@@ -182,7 +182,7 @@ def tile_qwen2attention_pa_kernel(
                         stop=(g == PASSES - 1),
                     )
             if kind == "F":
-                biased = work.tile([P, 512], F32, name="biased", tag="biased", bufs=6)
+                biased = work.tile([P, 512], F32, name="biased", tag="biased", bufs=8)
                 nc.scalar.activation(
                     out=biased[:], in_=acc[:], func=ACT.Identity, bias=zt32[:, 0, 4 * c + k : 4 * c + k + 1], scale=1.0
                 )
@@ -213,20 +213,22 @@ def tile_qwen2attention_pa_kernel(
                 )
             return prod
 
-        def finish(rnd, prod, span):
+        def rotated_bias(unit):
+            kind, c, k = unit
+            rb = auxp.tile([P, 512], F32, name="rb", tag="aux")
+            nc.tensor.matmul(
+                out=rb[:],
+                lhsT=lz[:, 2 + k, :],
+                rhs=rmat[c][:].rearrange("p h a j -> p (h a j)"),
+                start=True,
+                stop=True,
+            )
+            return rb
+
+        def finish(rnd, prod, span, rbs=()):
             o = work.tile([P, len(rnd), 512], F32, name="o", tag="o")
-            for j, unit in enumerate(rnd):
-                kind, c, k = unit
-                if kind == "T":
-                    rb = auxp.tile([P, 512], F32, name="rb", tag="aux")
-                    nc.tensor.matmul(
-                        out=rb[:],
-                        lhsT=lz[:, 2 + k, :],
-                        rhs=rmat[c][:].rearrange("p h a j -> p (h a j)"),
-                        start=True,
-                        stop=True,
-                    )
-                    nc.vector.tensor_tensor(out=prod[:, 0, j, :], in0=prod[:, 0, j, :], in1=rb[:], op=ALU.add)
+            for j, rb in enumerate(rbs):
+                nc.vector.tensor_tensor(out=prod[:, 0, j, :], in0=prod[:, 0, j, :], in1=rb[:], op=ALU.add)
             for j0 in range(0, len(rnd), span):
                 j1 = min(j0 + span, len(rnd))
                 nc.gpsimd.tensor_tensor(
@@ -263,7 +265,7 @@ def tile_qwen2attention_pa_kernel(
         build_rmat_vector(0)
 
         def value_heads(unit, src):
-            o = work.tile([P, 512], F32, name="ov", tag="ov")
+            o = work.tile([P, 512], F32, name="ov", tag="ov", bufs=4)
             nc.vector.tensor_tensor(out=o[:], in0=src[:], in1=bvb[:], op=ALU.add)
             nc.sync.dma_start(out=out_view(unit), in_=quarters(o[:]))
 
@@ -276,17 +278,22 @@ def tile_qwen2attention_pa_kernel(
         p1 = products(first[1], s1)
         x_quantize(2)
         s2 = [multiply(first[2][0])]
-        finish(first[0], p0, 1)
+        finish(first[0], p0, 1, [rotated_bias(first[0][0])])
         p2 = products(first[2], s2)
         x_quantize(3)
         s3 = [multiply(first[3][0])]
-        finish(first[1], p1, 1)
+        finish(first[1], p1, 1, [rotated_bias(first[1][0])])
 
         heads = [("F", c, k) for c in (1, 2, 3, 4) for k in range(4)]
-        rounds = [heads[j : j + ROUND] for j in range(0, len(heads), ROUND)]
-        srcs = [[multiply(unit) for unit in rounds[0]]]
+        rounds = []
+        for size in ROUND_SIZES:
+            done = sum(len(rnd) for rnd in rounds)
+            rounds.append(heads[done : done + size])
+        srcs = [[multiply(rounds[0][0])]]
         p3 = products(first[3], s3)
-        finish(first[2], p2, 1)
+        finish(first[2], p2, 1, [rotated_bias(first[2][0])])
+        srcs[0].append(multiply(rounds[0][1]))
+        finish(first[3], p3, 1, [rotated_bias(first[3][0])])
         bvp = auxp.tile([P, 512], F32, name="bvp", tag="aux")
         for hv in range(4):
             nc.tensor.matmul(
@@ -297,11 +304,11 @@ def tile_qwen2attention_pa_kernel(
                 stop=True,
             )
         nc.scalar.copy(out=bvb[:], in_=bvp[:])
+        srcs[0].extend([multiply(unit) for unit in rounds[0][2:]])
         for r in range(1, len(rounds)):
-            srcs.append([multiply(unit) for unit in rounds[r]])
-            if r == 1:
-                finish(first[3], p3, 1)
+            srcs.append([multiply(rounds[r][0])])
             finish(rounds[r - 1], products(rounds[r - 1], srcs[r - 1]), 2)
+            srcs[r].extend([multiply(unit) for unit in rounds[r][1:]])
         values = [("T", 5, m) for m in range(TOKEN_TILES)]
         for unit in values[0:2]:
             value_heads(unit, multiply(unit))

@@ -19,7 +19,7 @@ TOKEN_TILES = 4
 HALF = 64
 WARM_MATMULS = 5
 HOLD_MATMULS = 2
-ROUND_SIZES = (4, 4, 4, 2, 2)
+ROUND_SIZES = (1,) * 16
 
 FLOPS = 2 * 512 * 2048 * 3072
 
@@ -289,29 +289,36 @@ def tile_qwen2attention_pa_kernel(
         for size in ROUND_SIZES:
             done = sum(len(rnd) for rnd in rounds)
             rounds.append(heads[done : done + size])
-        srcs = [[multiply(rounds[0][0])]]
-        p3 = products(first[3], s3)
-        finish(first[2], p2, 1, [rotated_bias(first[2][0])])
-        srcs[0].append(multiply(rounds[0][1]))
-        finish(first[3], p3, 1, [rotated_bias(first[3][0])])
-        bvp = auxp.tile([P, 512], F32, name="bvp", tag="aux")
-        for hv in range(4):
-            nc.tensor.matmul(
-                out=bvp[:, P * hv : P * (hv + 1)],
-                lhsT=lz[:, 0, 20 + hv : 21 + hv].to_broadcast([P, P]),
-                rhs=ident_b[:],
-                start=True,
-                stop=True,
-            )
-        nc.scalar.copy(out=bvb[:], in_=bvp[:])
-        srcs[0].extend([multiply(unit) for unit in rounds[0][2:]])
-        for r in range(1, len(rounds)):
-            srcs.append([multiply(rounds[r][0])])
-            finish(rounds[r - 1], products(rounds[r - 1], srcs[r - 1]), 2)
-            srcs[r].extend([multiply(unit) for unit in rounds[r][1:]])
+        def spread_value_bias():
+            bvp = auxp.tile([P, 512], F32, name="bvp", tag="aux")
+            for hv in range(4):
+                nc.tensor.matmul(
+                    out=bvp[:, P * hv : P * (hv + 1)],
+                    lhsT=lz[:, 0, 20 + hv : 21 + hv].to_broadcast([P, P]),
+                    rhs=ident_b[:],
+                    start=True,
+                    stop=True,
+                )
+            nc.scalar.copy(out=bvb[:], in_=bvp[:])
+
+        src_of = {}
+        waiting = 0
+        for i, unit in enumerate(heads):
+            src_of[unit] = multiply(unit)
+            if i == 0:
+                p3 = products(first[3], s3)
+                finish(first[2], p2, 1, [rotated_bias(first[2][0])])
+            if i == 1:
+                finish(first[3], p3, 1, [rotated_bias(first[3][0])])
+                spread_value_bias()
+            if unit not in rounds[waiting]:
+                rnd = rounds[waiting]
+                finish(rnd, products(rnd, [src_of[u] for u in rnd]), 2)
+                waiting += 1
+        last = rounds[waiting]
         values = [("T", 5, m) for m in range(TOKEN_TILES)]
         for unit in values[0:2]:
             value_heads(unit, multiply(unit))
-        finish(rounds[-1], products(rounds[-1], srcs[-1]), 1)
+        finish(last, products(last, [src_of[u] for u in last]), 1)
         for unit in values[2:4]:
             value_heads(unit, multiply(unit))

@@ -19,7 +19,7 @@ TOKEN_TILES = 4
 HALF = 64
 WARM_MATMULS = 5
 HOLD_MATMULS = 2
-ROUND_SIZES = (1,) * 16
+ROUND_SIZES = (2,) * 8
 
 FLOPS = 2 * 512 * 2048 * 3072
 

@@ -18,7 +18,6 @@ PASSES = 4
 TOKEN_TILES = 4
 HALF = 64
 WARM_MATMULS = 5
-HOLD_MATMULS = 2
 ROUND_SIZES = (2,) * 8
 
 FLOPS = 2 * 512 * 2048 * 3072
@@ -56,7 +55,7 @@ def tile_qwen2attention_pa_kernel(
         zt32 = const.tile([P, 2, 32], F32, name="zt32")
         e01 = const.tile([P, 2, HALF], BF16, name="e01")
         rmat = {0: const.tile([P, 4, 2, HALF], BF16, name="rmat0")}
-        bvb = const.tile([P, 512], F32, name="bvb")
+        bvb = const.tile([P, 512], BF16, name="bvb")
         ident_f = const.tile([P, P], F32, name="ident_f")
         ident_b = const.tile([P, P], BF16, name="ident_b")
         warm_in = const.tile([P, 1], F32, name="warm_in")
@@ -104,6 +103,7 @@ def tile_qwen2attention_pa_kernel(
         load_plane(2)
         load_w(4)
         load_w(5)
+        nc.sync.dma_start(out=bvb[:], in_=bkv[512:1024].partition_broadcast(P))
 
         warm_ps = auxp.tile([P, 512], F32, name="warm_ps", tag="aux")
         for r in range(WARM_MATMULS):
@@ -243,9 +243,6 @@ def tile_qwen2attention_pa_kernel(
         nc.vector.tensor_tensor(out=e01[:, 0, :], in0=ident_b[:, 0:HALF], in1=ident_b[:, HALF:P], op=ALU.subtract)
         nc.vector.tensor_tensor(out=e01[:, 1, :], in0=ident_b[:, 0:HALF], in1=ident_b[:, HALF:P], op=ALU.add)
         x_transpose(0)
-        hold_ps = accp.tile([P, 512], F32, name="hold_ps", tag="acc")
-        for r in range(HOLD_MATMULS):
-            nc.tensor.matmul(out=hold_ps[:], lhsT=zeros[:, 0:P], rhs=zeros[:], start=True, stop=True)
         x_quantize(0)
         nc.vector.tensor_copy(out=tab[:, :, 0, 0:HALF], in_=tab[:, :, 0, HALF:P])
         nc.vector.tensor_scalar(out=tab[:, :, 1, HALF:P], in0=tab[:, :, 1, 0:HALF], scalar1=-1.0, scalar2=None, op0=ALU.mult)
@@ -253,7 +250,6 @@ def tile_qwen2attention_pa_kernel(
         nc.vector.tensor_copy(out=zswp[:, HALF:P], in_=zrow[:, 0:HALF])
         x_transpose(1)
         x_quantize(1)
-        early = [multiply(("T", 0, 0))]
 
         misc = auxp.tile([P, 6, P], BF16, name="misc", tag="aux")
         nc.tensor.transpose(misc[:, 0, :], zrow[:], ident_b[:])
@@ -270,7 +266,7 @@ def tile_qwen2attention_pa_kernel(
             nc.sync.dma_start(out=out_view(unit), in_=quarters(o[:]))
 
         first = [[("T", 0, m)] for m in range(TOKEN_TILES)]
-        s0 = early
+        s0 = [multiply(first[0][0])]
         x_transpose(2)
         s1 = [multiply(first[1][0])]
         x_transpose(3)
@@ -289,18 +285,6 @@ def tile_qwen2attention_pa_kernel(
         for size in ROUND_SIZES:
             done = sum(len(rnd) for rnd in rounds)
             rounds.append(heads[done : done + size])
-        def spread_value_bias():
-            bvp = auxp.tile([P, 512], F32, name="bvp", tag="aux")
-            for hv in range(4):
-                nc.tensor.matmul(
-                    out=bvp[:, P * hv : P * (hv + 1)],
-                    lhsT=lz[:, 0, 20 + hv : 21 + hv].to_broadcast([P, P]),
-                    rhs=ident_b[:],
-                    start=True,
-                    stop=True,
-                )
-            nc.scalar.copy(out=bvb[:], in_=bvp[:])
-
         src_of = {}
         waiting = 0
         for i, unit in enumerate(heads):
@@ -310,7 +294,6 @@ def tile_qwen2attention_pa_kernel(
                 finish(first[2], p2, 1, [rotated_bias(first[2][0])])
             if i == 1:
                 finish(first[3], p3, 1, [rotated_bias(first[3][0])])
-                spread_value_bias()
             if unit not in rounds[waiting]:
                 rnd = rounds[waiting]
                 finish(rnd, products(rnd, [src_of[u] for u in rnd]), 2)

@@ -32,22 +32,27 @@ def tile_qwen2attention_pa_kernel(
         work = ctx.enter_context(tc.tile_pool(name="work", bufs=3))
         accp = ctx.enter_context(tc.psum_pool(name="accp", bufs=4))
         auxp = ctx.enter_context(tc.psum_pool(name="auxp", bufs=4))
+        mxp = ctx.enter_context(tc.tile_pool(name="mxp", bufs=1))
         ctx.enter_context(tc.manual_schedule(engines={mybir.EngineType.PE}))
 
         plane_cols = (512, 1536, 1024)
+        plane_at = (0, 2048, 8192)
         planes = [
-            const.tile([P, PASSES, plane_cols[i]], U8, name="plane%d" % i, align_bytes=64) for i in range(3)
+            mxp.tile(
+                [P, PASSES, plane_cols[i]], U8, name="plane%d" % i, align_bytes=256 if i == 0 else 64, offset=plane_at[i]
+            )
+            for i in range(3)
         ]
         plane_src = (Wq_scales[:, :, 0:512], Wq_scales[:, :, 512:2048], Wkv_scales)
         plane_of = ((0, 0), (1, 0), (1, 512), (1, 1024), (2, 0), (2, 512))
-        w = [const.tile([P, PASSES, 1024], U8, name="w%d" % c, align_bytes=64) for c in range(6)]
+        w = [mxp.tile([P, PASSES, 1024], U8, name="w%d" % c, align_bytes=64, offset=12352 + 4096 * c) for c in range(6)]
         xs = [const.tile([P, 2048], BF16, name="xs%d" % m) for m in range(4)]
         grouped = [
             [const.tile([P, 1024], BF16, name="xg%d%d" % (m, gp), align_bytes=64) for gp in range(2)]
             for m in range(4)
         ]
-        xq = [const.tile([P, 512], U32, name="xq%d" % g, align_bytes=64) for g in range(PASSES)]
-        xsc = [const.tile([P, 512], U8, name="xc%d" % g, align_bytes=64) for g in range(PASSES)]
+        xq = [mxp.tile([P, 512], U32, name="xq%d" % g, align_bytes=64, offset=36992 + 2048 * g) for g in range(PASSES)]
+        xsc = [mxp.tile([P, 512], U8, name="xc%d" % g, align_bytes=64, offset=45248 + 512 * g) for g in range(PASSES)]
         tab = const.tile([P, TOKEN_TILES, 2, P], BF16, name="tab")
         zrow = const.tile([P, P], BF16, name="zrow")
         zswp = const.tile([P, P], BF16, name="zswp")

@@ -88,15 +88,15 @@ def tile_qwen2attention_pa_kernel(
             nc.sync.dma_start(out=w[c][:].bitcast(I32), in_=src.rearrange("g p b -> p g b").bitcast(I32))
 
         def load_x(queue, m):
-            queue.dma_start(out=xs[m][:], in_=x[0, P * m : P * (m + 1), :])
+            queue.dma_start(out=xs[m][:], in_=x[0].rearrange("(p m) k -> m p k", m=TOKEN_TILES)[m])
 
         load_x(nc.sync, 0)
         load_x(nc.scalar, 1)
-        nc.scalar.dma_start(out=tab[:, :, 0, HALF:P], in_=cos.rearrange("(m p) j -> p m j", p=P))
+        nc.scalar.dma_start(out=tab[:, :, 0, HALF:P], in_=cos.rearrange("(p m) j -> p m j", p=P))
         nc.scalar.activation(out=warm_out[:], in_=warm_in[:], func=ACT.Identity, bias=warm_in[:], scale=1.0)
         load_plane(0)
         load_w(0)
-        nc.sync.dma_start(out=tab[:, :, 1, 0:HALF], in_=sin.rearrange("(m p) j -> p m j", p=P))
+        nc.sync.dma_start(out=tab[:, :, 1, 0:HALF], in_=sin.rearrange("(p m) j -> p m j", p=P))
         nc.sync.dma_start(out=zrow[0:16, :], in_=bq.rearrange("(h f) -> h f", f=P))
         nc.sync.dma_start(out=zrow[16:24, :], in_=bkv.rearrange("(h f) -> h f", f=P))
         load_x(nc.sync, 2)
@@ -150,16 +150,15 @@ def tile_qwen2attention_pa_kernel(
         def out_view(unit):
             kind, c, k = unit
             if kind == "T":
-                rows = slice(P * k, P * (k + 1))
                 if c < 4:
-                    dst = out_0[0, 4 * c : 4 * c + 4, rows, :]
+                    dst = out_0[0, 4 * c : 4 * c + 4, :, :]
                 elif c == 4:
-                    dst = out_1[0, :, rows, :]
+                    dst = out_1[0, :, :, :]
                 else:
-                    dst = out_2[0, :, rows, :]
-                return dst.rearrange("h p d -> p h d")
+                    dst = out_2[0, :, :, :]
+                return dst.rearrange("h (p m) d -> m p h d", m=TOKEN_TILES)[k]
             dst = out_0[0, 4 * c + k, :, :] if c < 4 else out_1[0, k, :, :]
-            return dst.rearrange("(m p) d -> p m d", p=P)
+            return dst.rearrange("(p m) d -> p m d", p=P)
 
         def multiply(unit):
             kind, c, k = unit

@@ -33,7 +33,7 @@ def tile_qwen2attention_pa_kernel(
         accp = ctx.enter_context(tc.psum_pool(name="accp", bufs=4))
         auxp = ctx.enter_context(tc.psum_pool(name="auxp", bufs=4))
         mxp = ctx.enter_context(tc.tile_pool(name="mxp", bufs=1))
-        ctx.enter_context(tc.manual_schedule(engines={mybir.EngineType.PE}))
+        ctx.enter_context(tc.manual_schedule(engines={mybir.EngineType.PE, mybir.EngineType.SP}))
 
         plane_cols = (512, 1536, 1024)
         plane_at = (0, 2048, 8192)
@@ -45,7 +45,15 @@ def tile_qwen2attention_pa_kernel(
         ]
         plane_src = (Wq_scales[:, :, 0:512], Wq_scales[:, :, 512:2048], Wkv_scales)
         plane_of = ((0, 0), (1, 0), (1, 512), (1, 1024), (2, 0), (2, 512))
-        w = [mxp.tile([P, PASSES, 1024], U8, name="w%d" % c, align_bytes=64, offset=12352 + 4096 * c) for c in range(6)]
+        word_bytes = (1024, 1024, 2048, 2048)
+        word_at = (12352, 16448, 20544, 28736)
+        word_src = (Wq_words[:, :, 0:1024], Wq_words[:, :, 1024:2048], Wq_words[:, :, 2048:4096], Wkv_words)
+        word_of = ((0, 0), (1, 0), (2, 0), (2, 1024), (3, 0), (3, 1024))
+        w = [
+            mxp.tile([P, PASSES, word_bytes[i]], U8, name="w%d" % i, align_bytes=64, offset=word_at[i]) for i in range(4)
+        ]
+        o_first = const.tile([P, 4, TOKEN_TILES, P], F32, name="o_first")
+        v_pair = const.tile([P, 4, 2, P], F32, name="v_pair")
         xs = [const.tile([P, 2048], BF16, name="xs%d" % m) for m in range(4)]
         grouped = [
             [const.tile([P, 1024], BF16, name="xg%d%d" % (m, gp), align_bytes=64) for gp in range(2)]
@@ -83,9 +91,12 @@ def tile_qwen2attention_pa_kernel(
                     in_=plane_src[i][:, 4 * q : 4 * q + 4, :].rearrange("g r n -> r g n").bitcast(I32),
                 )
 
-        def load_w(c):
-            src = Wq_words[:, :, 1024 * c : 1024 * (c + 1)] if c < 4 else Wkv_words[:, :, 1024 * (c - 4) : 1024 * (c - 3)]
-            nc.sync.dma_start(out=w[c][:].bitcast(I32), in_=src.rearrange("g p b -> p g b").bitcast(I32))
+        def load_w(i):
+            nc.sync.dma_start(out=w[i][:].bitcast(I32), in_=word_src[i].rearrange("g p b -> p g b").bitcast(I32))
+
+        def words(c, g):
+            i, at = word_of[c]
+            return w[i][:, g, at : at + 1024]
 
         def load_x(queue, m):
             queue.dma_start(out=xs[m][:], in_=x[0].rearrange("(p m) k -> m p k", m=TOKEN_TILES)[m])
@@ -104,11 +115,6 @@ def tile_qwen2attention_pa_kernel(
         load_plane(1)
         load_w(1)
         load_w(2)
-        load_w(3)
-        load_plane(2)
-        load_w(4)
-        load_w(5)
-        nc.sync.dma_start(out=bvb[:], in_=bkv[512:1024].partition_broadcast(P))
 
         warm_ps = auxp.tile([P, 512], F32, name="warm_ps", tag="aux")
         for r in range(WARM_MATMULS):
@@ -170,7 +176,7 @@ def tile_qwen2attention_pa_kernel(
                         out=acc[:],
                         lhsT=xq[g][:, P * k : P * (k + 1)].bitcast(E5M2X4),
                         lhsT_scale=xsc[g][:, P * k : P * (k + 1)],
-                        rhs=w[c][:, g, :].bitcast(E2M1X4),
+                        rhs=words(c, g).bitcast(E2M1X4),
                         rhs_scale=planes[pl][:, g, off : off + 512],
                         start=(g == 0),
                         stop=(g == PASSES - 1),
@@ -178,7 +184,7 @@ def tile_qwen2attention_pa_kernel(
                 else:
                     nc.tensor.matmul_mx(
                         out=acc[:],
-                        lhsT=w[c][:, g, 256 * k : 256 * (k + 1)].bitcast(E2M1X4),
+                        lhsT=words(c, g)[:, 256 * k : 256 * (k + 1)].bitcast(E2M1X4),
                         lhsT_scale=planes[pl][:, g, off + P * k : off + P * (k + 1)],
                         rhs=xq[g][:].bitcast(E5M2X4),
                         rhs_scale=xsc[g][:],
@@ -229,12 +235,18 @@ def tile_qwen2attention_pa_kernel(
             )
             return rb
 
-        def finish(rnd, prod, span, rbs=()):
-            o = work.tile([P, len(rnd), 512], F32, name="o", tag="o")
-            for j, rb in enumerate(rbs):
-                nc.vector.tensor_tensor(out=prod[:, 0, j, :], in0=prod[:, 0, j, :], in1=rb[:], op=ALU.add)
-            for j0 in range(0, len(rnd), span):
-                j1 = min(j0 + span, len(rnd))
+        def finish_first(m, prod, rb):
+            nc.vector.tensor_tensor(out=prod[:, 0, 0, :], in0=prod[:, 0, 0, :], in1=rb[:], op=ALU.add)
+            nc.gpsimd.tensor_tensor(
+                out=o_first[:, :, m, :].rearrange("p h (a j) -> p h a j", j=HALF),
+                in0=prod[:, 0, 0, :].rearrange("p (h a j) -> p h a j", a=2, j=HALF),
+                in1=prod[:, 1, 0, :].rearrange("p (h a j) -> p h a j", a=2, j=HALF)[:, :, ::-1, :],
+                op=ALU.add,
+            )
+
+        def finish(rnd, prod, j_from, j_to):
+            o = work.tile([P, len(rnd), 512], F32, name="o", tag="o", bufs=5)
+            for j0, j1 in ((j_from, j_to),):
                 nc.gpsimd.tensor_tensor(
                     out=o[:, j0:j1, :].rearrange("p u (h a j) -> p (u h) a j", a=2, j=HALF),
                     in0=prod[:, 0, j0:j1, :].rearrange("p u (h a j) -> p (u h) a j", a=2, j=HALF),
@@ -278,11 +290,11 @@ def tile_qwen2attention_pa_kernel(
         p1 = products(first[1], s1)
         x_quantize(2)
         s2 = [multiply(first[2][0])]
-        finish(first[0], p0, 1, [rotated_bias(first[0][0])])
+        finish_first(0, p0, rotated_bias(first[0][0]))
         p2 = products(first[2], s2)
         x_quantize(3)
         s3 = [multiply(first[3][0])]
-        finish(first[1], p1, 1, [rotated_bias(first[1][0])])
+        finish_first(1, p1, rotated_bias(first[1][0]))
 
         heads = [("F", c, k) for c in (1, 2, 3, 4) for k in range(4)]
         rounds = []
@@ -295,17 +307,29 @@ def tile_qwen2attention_pa_kernel(
             src_of[unit] = multiply(unit)
             if i == 0:
                 p3 = products(first[3], s3)
-                finish(first[2], p2, 1, [rotated_bias(first[2][0])])
+                finish_first(2, p2, rotated_bias(first[2][0]))
             if i == 1:
-                finish(first[3], p3, 1, [rotated_bias(first[3][0])])
+                finish_first(3, p3, rotated_bias(first[3][0]))
+                nc.sync.dma_start(
+                    out=out_0[0, 0:4, :, :].rearrange("h (p m) d -> p h (m d)", m=TOKEN_TILES),
+                    in_=o_first[:].rearrange("p h m d -> p h (m d)"),
+                )
+                load_plane(2)
+                load_w(3)
+                nc.sync.dma_start(out=bvb[:], in_=bkv[512:1024].partition_broadcast(P))
             if unit not in rounds[waiting]:
                 rnd = rounds[waiting]
-                finish(rnd, products(rnd, [src_of[u] for u in rnd]), 2)
+                finish(rnd, products(rnd, [src_of[u] for u in rnd]), 0, len(rnd))
                 waiting += 1
         last = rounds[waiting]
         values = [("T", 5, m) for m in range(TOKEN_TILES)]
-        for unit in values[0:2]:
+        for m, unit in enumerate(values[0:2]):
+            nc.vector.tensor_tensor(out=v_pair[:, :, m, :], in0=quarters(multiply(unit)[:]), in1=quarters(bvb[:]), op=ALU.add)
+        nc.sync.dma_start(
+            out=out_2[0].rearrange("h (p m) d -> p h m d", m=TOKEN_TILES)[:, :, 0:2, :].rearrange("p h m d -> p h (m d)"),
+            in_=v_pair[:].rearrange("p h m d -> p h (m d)"),
+        )
+        p_last = products(last, [src_of[u] for u in last])
+        for j, unit in enumerate(values[2:4]):
             value_heads(unit, multiply(unit))
-        finish(last, products(last, [src_of[u] for u in last]), 1)
-        for unit in values[2:4]:
-            value_heads(unit, multiply(unit))
+            finish(last, p_last, j, j + 1)

from contextlib import ExitStack

import concourse.mybir as mybir
from concourse.masks import make_identity

F32 = mybir.dt.float32
BF16 = mybir.dt.bfloat16
I32 = mybir.dt.int32
U32 = mybir.dt.uint32
U8 = mybir.dt.uint8
E5M2X4 = mybir.dt.float8_e5m2_x4
E2M1X4 = mybir.dt.float4_e2m1fn_x4
ALU = mybir.AluOpType
ACT = mybir.ActivationFunctionType

P = 128
PASSES = 4
TOKEN_TILES = 4
HALF = 64
WARM_MATMULS = 5
ROUND_SIZES = (2,) * 8

FLOPS = 2 * 512 * 2048 * 3072


def tile_qwen2attention_pa_kernel(
    tc, x, Wq_words, Wq_scales, bq, Wkv_words, Wkv_scales, bkv, cos, sin, out_0, out_1, out_2
):
    nc = tc.nc
    with ExitStack() as ctx:
        const = ctx.enter_context(tc.tile_pool(name="const", bufs=1))
        work = ctx.enter_context(tc.tile_pool(name="work", bufs=3))
        accp = ctx.enter_context(tc.psum_pool(name="accp", bufs=4))
        auxp = ctx.enter_context(tc.psum_pool(name="auxp", bufs=4))
        mxp = ctx.enter_context(tc.tile_pool(name="mxp", bufs=1))
        ctx.enter_context(tc.manual_schedule(engines={mybir.EngineType.PE, mybir.EngineType.SP}))

        plane_cols = (512, 1536, 1024)
        plane_at = (0, 2048, 8192)
        planes = [
            mxp.tile(
                [P, PASSES, plane_cols[i]], U8, name="plane%d" % i, align_bytes=256 if i == 0 else 64, offset=plane_at[i]
            )
            for i in range(3)
        ]
        plane_src = (Wq_scales[:, :, 0:512], Wq_scales[:, :, 512:2048], Wkv_scales)
        plane_of = ((0, 0), (1, 0), (1, 512), (1, 1024), (2, 0), (2, 512))
        word_bytes = (1024, 1024, 2048, 2048)
        word_at = (12352, 16448, 20544, 28736)
        word_src = (Wq_words[:, :, 0:1024], Wq_words[:, :, 1024:2048], Wq_words[:, :, 2048:4096], Wkv_words)
        word_of = ((0, 0), (1, 0), (2, 0), (2, 1024), (3, 0), (3, 1024))
        w = [
            mxp.tile([P, PASSES, word_bytes[i]], U8, name="w%d" % i, align_bytes=64, offset=word_at[i]) for i in range(4)
        ]
        o_first = const.tile([P, 4, TOKEN_TILES, P], F32, name="o_first")
        v_pair = const.tile([P, 4, 2, P], F32, name="v_pair")
        xs = [const.tile([P, 2048], BF16, name="xs%d" % m) for m in range(4)]
        grouped = [
            [const.tile([P, 1024], BF16, name="xg%d%d" % (m, gp), align_bytes=64) for gp in range(2)]
            for m in range(4)
        ]
        xq = [mxp.tile([P, 512], U32, name="xq%d" % g, align_bytes=64, offset=36992 + 2048 * g) for g in range(PASSES)]
        xsc = [mxp.tile([P, 512], U8, name="xc%d" % g, align_bytes=64, offset=45248 + 512 * g) for g in range(PASSES)]
        tab = const.tile([P, TOKEN_TILES, 2, P], BF16, name="tab")
        zrow = const.tile([P, P], BF16, name="zrow")
        zswp = const.tile([P, P], BF16, name="zswp")
        lz = const.tile([P, 6, P], BF16, name="lz")
        zt32 = const.tile([P, 2, 32], F32, name="zt32")
        e01 = const.tile([P, 2, HALF], BF16, name="e01")
        rmat = {0: const.tile([P, 4, 2, HALF], BF16, name="rmat0")}
        bvb = const.tile([P, 512], BF16, name="bvb")
        ident_f = const.tile([P, P], F32, name="ident_f")
        ident_b = const.tile([P, P], BF16, name="ident_b")
        warm_in = const.tile([P, 1], F32, name="warm_in")
        warm_out = const.tile([P, 1], F32, name="warm_out")
        zeros = const.tile([P, 512], BF16, name="zeros")

        nc.gpsimd.memset(zeros[:], 0.0)
        nc.vector.memset(planes[0][:].bitcast(I32), 0)
        nc.vector.memset(warm_in[:], 0.0)
        nc.vector.memset(zrow[:], 0.0)
        nc.vector.memset(planes[1][:].bitcast(I32), 0)
        nc.vector.memset(planes[2][:].bitcast(I32), 0)
        make_identity(nc, ident_f[:])
        make_identity(nc, ident_b[:])

        def load_plane(i):
            for q in range(4):
                nc.sync.dma_start(
                    out=planes[i][32 * q : 32 * q + 4, :, :].bitcast(I32),
                    in_=plane_src[i][:, 4 * q : 4 * q + 4, :].rearrange("g r n -> r g n").bitcast(I32),
                )

        def load_w(i):
            nc.sync.dma_start(out=w[i][:].bitcast(I32), in_=word_src[i].rearrange("g p b -> p g b").bitcast(I32))

        def words(c, g):
            i, at = word_of[c]
            return w[i][:, g, at : at + 1024]

        def load_x(queue, m):
            queue.dma_start(out=xs[m][:], in_=x[0].rearrange("(p m) k -> m p k", m=TOKEN_TILES)[m])

        load_x(nc.sync, 0)
        load_x(nc.scalar, 1)
        nc.scalar.dma_start(out=tab[:, :, 0, HALF:P], in_=cos.rearrange("(p m) j -> p m j", p=P))
        nc.scalar.activation(out=warm_out[:], in_=warm_in[:], func=ACT.Identity, bias=warm_in[:], scale=1.0)
        load_plane(0)
        load_w(0)
        nc.sync.dma_start(out=tab[:, :, 1, 0:HALF], in_=sin.rearrange("(p m) j -> p m j", p=P))
        nc.sync.dma_start(out=zrow[0:16, :], in_=bq.rearrange("(h f) -> h f", f=P))
        nc.sync.dma_start(out=zrow[16:24, :], in_=bkv.rearrange("(h f) -> h f", f=P))
        load_x(nc.sync, 2)
        load_x(nc.sync, 3)
        load_plane(1)
        load_w(1)
        load_w(2)

        warm_ps = auxp.tile([P, 512], F32, name="warm_ps", tag="aux")
        for r in range(WARM_MATMULS):
            nc.tensor.matmul(out=warm_ps[:], lhsT=zeros[:, 0:P], rhs=zeros[:], start=True, stop=True)

        def x_transpose(m):
            for gp in range(2):
                words = xs[m][:, 1024 * gp : 1024 * (gp + 1)].bitcast(F32)
                xt = auxp.tile([P, 2, 2, P], F32, name="xt", tag="aux")
                for gl in range(2):
                    for u in range(2):
                        nc.tensor.transpose(xt[:, gl, u, :], words[:, 256 * gl + u : 256 * (gl + 1) : 2], ident_f[:])
                nc.scalar.copy(
                    out=grouped[m][gp][:].bitcast(F32).rearrange("p (g r u) -> p g r u", g=2, u=2),
                    in_=xt[:].rearrange("p g u r -> p g r u"),
                )

        def x_quantize(m):
            for g in range(PASSES):
                gp, gl = divmod(g, 2)
                nc.vector.quantize_mx(
                    out=xq[g][:, P * m : P * (m + 1)].bitcast(E5M2X4),
                    scales=xsc[g][:, P * m : P * (m + 1)],
                    in_=grouped[m][gp][:, 512 * gl : 512 * (gl + 1)],
                )

        def build_rmat_vector(c):
            for a in range(2):
                nc.vector.tensor_tensor(
                    out=rmat[c][:, :, a, :],
                    in0=e01[:, a : a + 1, :].to_broadcast([P, 4, HALF]),
                    in1=lz[:, a, 4 * c : 4 * c + 4].unsqueeze(2).to_broadcast([P, 4, HALF]),
                    op=ALU.mult,
                )

        def quarters(ap):
            return ap.rearrange("p (h f) -> p h f", f=P)

        def out_view(unit):
            kind, c, k = unit
            if kind == "T":
                if c < 4:
                    dst = out_0[0, 4 * c : 4 * c + 4, :, :]
                elif c == 4:
                    dst = out_1[0, :, :, :]
                else:
                    dst = out_2[0, :, :, :]
                return dst.rearrange("h (p m) d -> m p h d", m=TOKEN_TILES)[k]
            dst = out_0[0, 4 * c + k, :, :] if c < 4 else out_1[0, k, :, :]
            return dst.rearrange("(p m) d -> p m d", p=P)

        def multiply(unit):
            kind, c, k = unit
            acc = accp.tile([P, 512], F32, name="acc", tag="acc")
            pl, off = plane_of[c]
            for g in range(PASSES):
                if kind == "T":
                    nc.tensor.matmul_mx(
                        out=acc[:],
                        lhsT=xq[g][:, P * k : P * (k + 1)].bitcast(E5M2X4),
                        lhsT_scale=xsc[g][:, P * k : P * (k + 1)],
                        rhs=words(c, g).bitcast(E2M1X4),
                        rhs_scale=planes[pl][:, g, off : off + 512],
                        start=(g == 0),
                        stop=(g == PASSES - 1),
                    )
                else:
                    nc.tensor.matmul_mx(
                        out=acc[:],
                        lhsT=words(c, g)[:, 256 * k : 256 * (k + 1)].bitcast(E2M1X4),
                        lhsT_scale=planes[pl][:, g, off + P * k : off + P * (k + 1)],
                        rhs=xq[g][:].bitcast(E5M2X4),
                        rhs_scale=xsc[g][:],
                        start=(g == 0),
                        stop=(g == PASSES - 1),
                    )
            if kind == "F":
                biased = work.tile([P, 512], F32, name="biased", tag="biased", bufs=8)
                nc.scalar.activation(
                    out=biased[:], in_=acc[:], func=ACT.Identity, bias=zt32[:, 0, 4 * c + k : 4 * c + k + 1], scale=1.0
                )
                return biased
            return acc

        def products(rnd, srcs):
            ins = []
            for unit, src in zip(rnd, srcs):
                if unit[0] == "F":
                    back = auxp.tile([P, 512], F32, name="back", tag="aux")
                    for m in range(TOKEN_TILES):
                        nc.tensor.transpose(back[:, P * m : P * (m + 1)], src[:, P * m : P * (m + 1)], ident_f[:])
                    ins.append(back)
                else:
                    ins.append(src)
            prod = work.tile([P, 2, len(rnd), 512], F32, name="prod", tag="prod")
            for j, unit in enumerate(rnd):
                if unit[0] == "T":
                    table = tab[:, unit[2], :, :].unsqueeze(2).to_broadcast([P, 2, 4, P])
                else:
                    table = tab[:].rearrange("p m t f -> p t m f")
                nc.vector.tensor_tensor(
                    out=prod[:, :, j, :].rearrange("p t (h f) -> p t h f", f=P),
                    in0=quarters(ins[j][:]).unsqueeze(1).to_broadcast([P, 2, 4, P]),
                    in1=table,
                    op=ALU.mult,
                )
            return prod

        def rotated_bias(unit):
            kind, c, k = unit
            rb = auxp.tile([P, 512], F32, name="rb", tag="aux")
            nc.tensor.matmul(
                out=rb[:],
                lhsT=lz[:, 2 + k, :],
                rhs=rmat[c][:].rearrange("p h a j -> p (h a j)"),
                start=True,
                stop=True,
            )
            return rb

        def finish_first(m, prod, rb):
            nc.vector.tensor_tensor(out=prod[:, 0, 0, :], in0=prod[:, 0, 0, :], in1=rb[:], op=ALU.add)
            nc.gpsimd.tensor_tensor(
                out=o_first[:, :, m, :].rearrange("p h (a j) -> p h a j", j=HALF),
                in0=prod[:, 0, 0, :].rearrange("p (h a j) -> p h a j", a=2, j=HALF),
                in1=prod[:, 1, 0, :].rearrange("p (h a j) -> p h a j", a=2, j=HALF)[:, :, ::-1, :],
                op=ALU.add,
            )

        def finish(rnd, prod, j_from, j_to):
            o = work.tile([P, len(rnd), 512], F32, name="o", tag="o", bufs=5)
            for j0, j1 in ((j_from, j_to),):
                nc.gpsimd.tensor_tensor(
                    out=o[:, j0:j1, :].rearrange("p u (h a j) -> p (u h) a j", a=2, j=HALF),
                    in0=prod[:, 0, j0:j1, :].rearrange("p u (h a j) -> p (u h) a j", a=2, j=HALF),
                    in1=prod[:, 1, j0:j1, :].rearrange("p u (h a j) -> p (u h) a j", a=2, j=HALF)[:, :, ::-1, :],
                    op=ALU.add,
                )
                for j in range(j0, j1):
                    nc.sync.dma_start(out=out_view(rnd[j]), in_=quarters(o[:, j, :]))

        nc.vector.tensor_tensor(out=e01[:, 0, :], in0=ident_b[:, 0:HALF], in1=ident_b[:, HALF:P], op=ALU.subtract)
        nc.vector.tensor_tensor(out=e01[:, 1, :], in0=ident_b[:, 0:HALF], in1=ident_b[:, HALF:P], op=ALU.add)
        x_transpose(0)
        x_quantize(0)
        nc.vector.tensor_copy(out=tab[:, :, 0, 0:HALF], in_=tab[:, :, 0, HALF:P])
        nc.vector.tensor_scalar(out=tab[:, :, 1, HALF:P], in0=tab[:, :, 1, 0:HALF], scalar1=-1.0, scalar2=None, op0=ALU.mult)
        nc.vector.tensor_copy(out=zswp[:, 0:HALF], in_=zrow[:, HALF:P])
        nc.vector.tensor_copy(out=zswp[:, HALF:P], in_=zrow[:, 0:HALF])
        x_transpose(1)
        x_quantize(1)

        misc = auxp.tile([P, 6, P], BF16, name="misc", tag="aux")
        nc.tensor.transpose(misc[:, 0, :], zrow[:], ident_b[:])
        nc.tensor.transpose(misc[:, 1, :], zswp[:], ident_b[:])
        for m in range(TOKEN_TILES):
            nc.tensor.transpose(misc[:, 2 + m, :], tab[:, m, :, :].rearrange("p t f -> p (t f)")[:, HALF : HALF + P], ident_b[:])
        nc.vector.tensor_copy(out=lz[:], in_=misc[:])
        nc.vector.tensor_copy(out=zt32[:], in_=misc[:, 0:2, 0:32])
        build_rmat_vector(0)

        def value_heads(unit, src):
            o = work.tile([P, 512], F32, name="ov", tag="ov", bufs=4)
            nc.vector.tensor_tensor(out=o[:], in0=src[:], in1=bvb[:], op=ALU.add)
            nc.sync.dma_start(out=out_view(unit), in_=quarters(o[:]))

        first = [[("T", 0, m)] for m in range(TOKEN_TILES)]
        s0 = [multiply(first[0][0])]
        x_transpose(2)
        s1 = [multiply(first[1][0])]
        x_transpose(3)
        p0 = products(first[0], s0)
        p1 = products(first[1], s1)
        x_quantize(2)
        s2 = [multiply(first[2][0])]
        finish_first(0, p0, rotated_bias(first[0][0]))
        p2 = products(first[2], s2)
        x_quantize(3)
        s3 = [multiply(first[3][0])]
        finish_first(1, p1, rotated_bias(first[1][0]))

        heads = [("F", c, k) for c in (1, 2, 3, 4) for k in range(4)]
        rounds = []
        for size in ROUND_SIZES:
            done = sum(len(rnd) for rnd in rounds)
            rounds.append(heads[done : done + size])
        src_of = {}
        waiting = 0
        for i, unit in enumerate(heads):
            src_of[unit] = multiply(unit)
            if i == 0:
                p3 = products(first[3], s3)
                finish_first(2, p2, rotated_bias(first[2][0]))
            if i == 1:
                finish_first(3, p3, rotated_bias(first[3][0]))
                nc.sync.dma_start(
                    out=out_0[0, 0:4, :, :].rearrange("h (p m) d -> p h (m d)", m=TOKEN_TILES),
                    in_=o_first[:].rearrange("p h m d -> p h (m d)"),
                )
                load_plane(2)
                load_w(3)
                nc.sync.dma_start(out=bvb[:], in_=bkv[512:1024].partition_broadcast(P))
            if unit not in rounds[waiting]:
                rnd = rounds[waiting]
                finish(rnd, products(rnd, [src_of[u] for u in rnd]), 0, len(rnd))
                waiting += 1
        last = rounds[waiting]
        values = [("T", 5, m) for m in range(TOKEN_TILES)]
        for m, unit in enumerate(values[0:2]):
            nc.vector.tensor_tensor(out=v_pair[:, :, m, :], in0=quarters(multiply(unit)[:]), in1=quarters(bvb[:]), op=ALU.add)
        nc.sync.dma_start(
            out=out_2[0].rearrange("h (p m) d -> p h m d", m=TOKEN_TILES)[:, :, 0:2, :].rearrange("p h m d -> p h (m d)"),
            in_=v_pair[:].rearrange("p h m d -> p h (m d)"),
        )
        p_last = products(last, [src_of[u] for u in last])
        for j, unit in enumerate(values[2:4]):
            value_heads(unit, multiply(unit))
            finish(last, p_last, j, j + 1)
